import numpy as np
import ml_dtypes


def mxq(x, axis, fmt="e4m3"):
    dtype, down = {"e4m3": (ml_dtypes.float8_e4m3fn, 7), "e5m2": (ml_dtypes.float8_e5m2, 14)}[fmt]
    v = np.moveaxis(np.asarray(x, np.float32).astype(ml_dtypes.bfloat16).astype(np.float64), axis, -1)
    blocks = v.reshape(v.shape[:-1] + (-1, 32))
    amax = np.abs(blocks).max(-1, keepdims=True)
    byte = np.maximum(np.where(amax > 0, np.frexp(amax)[1] - 1 + 127, 0) - down, 1)
    scale = np.exp2(byte - 127.0)
    codes = (blocks / scale).astype(np.float32).astype(dtype).astype(np.float64)
    return np.moveaxis((codes * scale).reshape(v.shape), -1, axis)


WIDE = False


def mx_kscale(k):
    if not WIDE:
        return np.ones(k)
    levels = np.array([10, -10, 5, -5, 0])
    if k % 512:
        return np.exp2(np.random.permutation(np.resize(levels, k // 32))).repeat(32)
    a = np.empty((k // 512, 16))
    for p in range(k // 512):
        a[p, :8] = np.random.permutation(np.resize(levels, 8))
        for g in range(8):
            far = levels[np.abs(levels - a[p, g]) >= 10]
            a[p, g + 8] = far[np.random.randint(len(far))]
    return np.exp2(a.ravel()).repeat(32)


BF16 = ml_dtypes.bfloat16


def bf(x):
    return np.asarray(x, np.float32).astype(BF16)


def f64(x):
    return np.asarray(x).astype(np.float64)


B, N, HD, ED, F = 1, 80, 512, 1024, 2048
TD = HD + HD
MD = TD + ED
EPS = 1e-5


def layer_norm(x, g, b):
    mu = x.mean(-1, keepdims=True)
    var = x.var(-1, keepdims=True)
    return (x - mu) * (1.0 / np.sqrt(var + EPS)) * g + b


def setup_inputs():
    t = mx_kscale(F)
    rx = mx_kscale(MD)[:HD]
    r = np.concatenate([rx, rx, np.ones(ED)])
    return {"hid": bf(np.maximum(np.random.standard_normal((B, N, N, F)), 0.0) * t),
            "x_down": bf(np.random.standard_normal((B, N, HD)) * rx),
            "p_ln": bf(np.random.standard_normal((B, N, N, ED))),
            "W2": bf(np.random.standard_normal((F, MD)) / np.sqrt(F) / t[:, None] * r),
            "b2": bf(0.1 * np.random.standard_normal(MD) * r),
            "Wo": bf(np.random.standard_normal((MD, ED)) / np.sqrt(MD) / r[:, None]),
            "bo": bf(0.1 * np.random.standard_normal(ED)),
            "ln_out_g": bf(1.0 + 0.1 * np.random.standard_normal(ED)),
            "ln_out_b": bf(0.1 * np.random.standard_normal(ED))}


def reference(hid, x_down, p_ln, W2, b2, Wo, bo, ln_out_g, ln_out_b):
    xd, pl = f64(x_down), f64(p_ln)
    edge_bias = np.concatenate([np.broadcast_to(xd[:, :, None, :], (B, N, N, HD)),
                                np.broadcast_to(xd[:, None, :, :], (B, N, N, HD))], axis=-1)
    z_in = np.concatenate([edge_bias, pl], axis=-1)
    m = np.maximum((mxq(f64(hid), 3, "e4m3") @ mxq(f64(W2), 0, "e4m3")) + f64(b2), 0.0)
    z = (mxq(m + z_in, 3, "e4m3") @ mxq(f64(Wo), 0, "e4m3")) + f64(bo)
    return pl + layer_norm(z, f64(ln_out_g), f64(ln_out_b))

@@ -1,0 +1,525 @@
+from contextlib import ExitStack
+
+import concourse.mybir as mybir
+from concourse.masks import make_identity
+
+F32 = mybir.dt.float32
+BF16 = mybir.dt.bfloat16
+U32 = mybir.dt.uint32
+U8 = mybir.dt.uint8
+FP8X4 = mybir.dt.float8_e4m3fn_x4
+ALU = mybir.AluOpType
+ACT = mybir.ActivationFunctionType
+
+P = 128
+NODES = 80
+TOKENS = NODES * NODES
+F_IN = 2048
+MD = 2048
+ED = 1024
+EPS = 1e-5
+TB = 256
+NB = TOKENS // TB
+KP = 4
+NG = 4
+W_AHEAD = 5
+W_ON_VECTOR = ()
+
+FLOPS = 2 * TOKENS * F_IN * MD + 2 * TOKENS * MD * ED
+
+
+def tile_edgeupdaterwrapper_v01_pb_l_kernel(tc, hid, x_down, p_ln, W2, b2, Wo, bo, ln_out_g, ln_out_b, out):
+    nc = tc.nc
+    hid_rows = hid.flatten_outer_dims()
+    pln_rows = p_ln.flatten_outer_dims()
+    out_rows = out.flatten_outer_dims()
+    xd_rows = x_down.flatten_outer_dims()
+
+    with ExitStack() as ctx:
+        keep = ctx.enter_context(tc.tile_pool(name="keep", bufs=1))
+        wst = ctx.enter_context(tc.tile_pool(name="wst", bufs=3))
+        st = ctx.enter_context(tc.tile_pool(name="st", bufs=2))
+        psum = ctx.enter_context(tc.psum_pool(name="psum", bufs=8))
+        ctx.enter_context(tc.manual_schedule())
+
+        w2c = keep.tile([P, KP, MD], U32, name="w2c", align_bytes=64)
+        w2s = keep.tile([P, KP, MD], U8, name="w2s", align_bytes=64)
+        woc = keep.tile([P, NG, ED], U32, name="woc", align_bytes=64)
+        wos = keep.tile([P, NG, ED], U8, name="wos", align_bytes=64)
+        ident = keep.tile([P, P], F32, name="ident")
+        ones = keep.tile([P, P], BF16, name="ones")
+        crow = keep.tile([P, 3 * ED], BF16, name="crow")
+        cbc = keep.tile([P, 3, ED], BF16, name="cbc")
+        b2raw = keep.tile([P, NG, 4], BF16, name="b2raw")
+        b2f = keep.tile([P, NG * 4], F32, name="b2f")
+        negb2 = keep.tile([P, NG * 4], F32, name="negb2")
+        xdraw = keep.tile([P, 512], BF16, name="xdraw")
+        xi = keep.tile([P, 4, NODES], F32, name="xi")
+        xj = keep.tile([P, 4, 4 * NODES + 16], F32, name="xj")
+        eps = keep.tile([P, 1], F32, name="eps")
+        warm = keep.tile([P, 1], F32, name="warm")
+
+        live = {}
+
+        def bank(nm):
+            return psum.tile([P, 512], F32, name=nm, tag="bank")
+
+        def ok(b):
+            return 0 <= b < NB
+
+        def load_h(b):
+            if not ok(b):
+                return
+            for i in range(2):
+                t = st.tile([P, F_IN], BF16, name="hraw", tag="hraw", bufs=4)
+                r0 = b * TB + i * P
+                nc.sync.dma_start(out=t[:], in_=hid_rows[r0:r0 + P, :])
+                live[("hraw", b, i)] = t
+
+        def load_p(b):
+            if not ok(b):
+                return
+            for i in range(2):
+                t = st.tile([P, ED], BF16, name="praw", tag="praw", bufs=6)
+                r0 = b * TB + i * P
+                nc.sync.dma_start(out=t[:], in_=pln_rows[r0:r0 + P, :])
+                live[("praw", b, i)] = t
+
+        def tr_bank(b, kind, c):
+            pt = bank("tp")
+            for u in range(2):
+                for i in range(2):
+                    words = live[(kind, b, i)][:].bitcast(F32)
+                    nc.tensor.transpose(pt[:, u * TB + i * P:u * TB + (i + 1) * P],
+                                        words[:, 256 * c + u:256 * (c + 1):2], ident[:])
+            live[("tp", kind, b, c)] = pt
+
+        def tr1(b):
+            if not ok(b):
+                return
+            for c in range(3):
+                tr_bank(b, "hraw", c)
+
+        def tr2(b):
+            if not ok(b):
+                return
+            tr_bank(b, "hraw", 3)
+            tr_bank(b, "praw", 0)
+            tr_bank(b, "praw", 1)
+
+        def cp(b, c):
+            if not ok(b):
+                return
+            pt = live.pop(("tp", "hraw", b, c))
+            hg = st.tile([P, 4 * TB], BF16, name="hg", tag="hg", bufs=4, align_bytes=64)
+            nc.scalar.copy(out=hg[:].bitcast(F32).rearrange("p (n u) -> p n u", u=2),
+                           in_=pt[:].rearrange("p (u n) -> p n u", u=2))
+            live[("hg", b, c)] = hg
+
+        def qh(b, c):
+            if not ok(b):
+                return
+            if c == 0:
+                live[("hc", b)] = st.tile([P, KP, TB], U32, name="hc", tag="hc", bufs=2, align_bytes=64)
+                live[("hs", b)] = st.tile([P, KP, TB], U8, name="hs", tag="hs", bufs=2, align_bytes=64)
+            hg = live.pop(("hg", b, c))
+            nc.vector.quantize_mx(out=live[("hc", b)][:, c, :].bitcast(FP8X4), scales=live[("hs", b)][:, c, :], in_=hg[:])
+
+        def xp(b):
+            if not ok(b):
+                return
+            x = st.tile([P, 2, 4, TB], F32, name="xp", tag="xp", bufs=2)
+            for c in range(2):
+                pt = live.pop(("tp", "praw", b, c))
+                v = pt[:].bitcast(BF16).rearrange("p (u n e) -> p u n e", u=2, e=2)
+                for u in range(2):
+                    for e in range(2):
+                        t = 2 * u + e
+                        col = 4 * (2 + c) + t
+                        nc.scalar.activation(out=x[:, c, t, :], in_=v[:, u, :, e], func=ACT.Identity,
+                                             bias=b2f[:, col:col + 1], scale=1.0)
+            live[("xp", b)] = x
+
+        def m1(b, g):
+            if not ok(b):
+                return
+            hc = live[("hc", b)]
+            hs = live[("hs", b)]
+            for k in range(2):
+                pt = bank("s1")
+                for h in range(2):
+                    c0 = 512 * g + P * (2 * k + h)
+                    for c in range(KP):
+                        nc.tensor.matmul_mx(out=pt[:, h * TB:(h + 1) * TB],
+                                            lhsT=w2c[:, c, c0:c0 + P].bitcast(FP8X4), lhsT_scale=w2s[:, c, c0:c0 + P],
+                                            rhs=hc[:, c, :].bitcast(FP8X4), rhs_scale=hs[:, c, :],
+                                            start=(c == 0), stop=(c == KP - 1))
+                live[("s1", b, g, k)] = pt
+
+        def stt(b, g, k):
+            if not ok(b):
+                return
+            if k == 0:
+                live[("sp", b, g)] = st.tile([P, 4, TB], BF16, name="sp", tag="sp", bufs=3)
+            sp = live[("sp", b, g)]
+            pt = live.pop(("s1", b, g, k))
+            for h in range(2):
+                t = 2 * k + h
+                col = 4 * g + t
+                if g == 0:
+                    lo = 0
+                    while lo < TB:
+                        i = (b * TB + lo) // NODES
+                        hi = min(TB, (i + 1) * NODES - b * TB)
+                        nc.vector.tensor_scalar(out=sp[:, t, lo:hi], in0=pt[:, h * TB + lo:h * TB + hi],
+                                                scalar1=negb2[:, col:col + 1], scalar2=xi[:, t, i:i + 1],
+                                                op0=ALU.max, op1=ALU.add)
+                        lo = hi
+                else:
+                    if g == 1:
+                        off = (b * TB) % NODES
+                        x = xj[:, t, off:off + TB]
+                    else:
+                        x = live[("xp", b)][:, g - 2, t, :]
+                    nc.vector.scalar_tensor_tensor(out=sp[:, t, :], in0=pt[:, h * TB:(h + 1) * TB],
+                                                   scalar=negb2[:, col:col + 1], in1=x, op0=ALU.max, op1=ALU.add)
+
+        def il(b, g):
+            if not ok(b):
+                return
+            sp = live.pop(("sp", b, g))
+            sg = st.tile([P, TB, 4], BF16, name="sg", tag="sg", bufs=3, align_bytes=64)
+            nc.scalar.copy(out=sg[:], in_=sp[:].rearrange("p t n -> p n t"))
+            live[("sg", b, g)] = sg
+
+        def qs(b, g):
+            if not ok(b):
+                return
+            if g == 0:
+                live[("sc", b)] = st.tile([P, NG, TB], U32, name="sc", tag="sc", bufs=2, align_bytes=64)
+                live[("ss", b)] = st.tile([P, NG, TB], U8, name="ss", tag="ss", bufs=2, align_bytes=64)
+            sg = live.pop(("sg", b, g))
+            nc.vector.quantize_mx(out=live[("sc", b)][:, g, :].bitcast(FP8X4), scales=live[("ss", b)][:, g, :],
+                                  in_=sg[:].rearrange("p n t -> p (n t)"))
+
+        def m2(b, i):
+            if not ok(b):
+                return
+            sc = live[("sc", b)]
+            ss = live[("ss", b)]
+            for h in range(2):
+                pt = bank("s2")
+                for g in range(NG):
+                    nc.tensor.matmul_mx(out=pt[:], lhsT=sc[:, g, i * P:(i + 1) * P].bitcast(FP8X4),
+                                        lhsT_scale=ss[:, g, i * P:(i + 1) * P],
+                                        rhs=woc[:, g, h * 512:(h + 1) * 512].bitcast(FP8X4),
+                                        rhs_scale=wos[:, g, h * 512:(h + 1) * 512],
+                                        start=(g == 0), stop=(g == NG - 1))
+                live[("s2", b, i, h)] = pt
+
+        def i1(b, i, h):
+            if not ok(b):
+                return
+            if h == 0:
+                live[("z", b, i)] = st.tile([P, ED], F32, name="z", tag="z", bufs=2)
+                live[("zs", b, i)] = st.tile([P, 2], F32, name="zs", tag="zs", bufs=3)
+            pt = live.pop(("s2", b, i, h))
+            nc.vector.scalar_tensor_tensor(out=live[("z", b, i)][:, h * 512:(h + 1) * 512], in0=pt[:], scalar=1.0,
+                                           in1=cbc[:, 0, h * 512:(h + 1) * 512], op0=ALU.mult, op1=ALU.add,
+                                           accum_out=live[("zs", b, i)][:, h:h + 1])
+
+        def negmu(b, i):
+            if not ok(b):
+                return
+            nm = st.tile([P, 1], F32, name="nm", tag="nm", bufs=3)
+            zs = live.pop(("zs", b, i))
+            nc.vector.tensor_scalar(out=nm[:], in0=zs[:, 0:1], scalar1=zs[:, 1:2], scalar2=-1.0 / ED,
+                                    op0=ALU.add, op1=ALU.mult)
+            live[("nm", b, i)] = nm
+
+        def i3(b, i):
+            if not ok(b):
+                return
+            y = st.tile([P, ED], F32, name="y", tag="y", bufs=3)
+            nc.vector.scalar_tensor_tensor(out=y[:], in0=live[("z", b, i)][:], scalar=live[("nm", b, i)][:],
+                                           in1=cbc[:, 1, :], op0=ALU.add, op1=ALU.mult)
+            live[("y", b, i)] = y
+
+        def sq(b, i):
+            if not ok(b):
+                return
+            junk = st.tile([P, ED], BF16, name="junk", tag="junk", bufs=1)
+            ssq = st.tile([P, 1], F32, name="ssq", tag="ssq", bufs=3)
+            sd = st.tile([P, 1], F32, name="sd", tag="sd", bufs=3)
+            nc.scalar.activation(out=junk[:], in_=live.pop(("z", b, i))[:], func=ACT.Square,
+                                 bias=live.pop(("nm", b, i))[:], scale=1.0, accum_out=ssq[:])
+            nc.scalar.activation(out=sd[:], in_=ssq[:], func=ACT.Sqrt, bias=eps[:], scale=1.0 / ED)
+            live[("sd", b, i)] = sd
+
+        def qadd(b, i):
+            if not ok(b):
+                return
+            q = st.tile([P, ED], F32, name="q", tag="q", bufs=2)
+            nc.gpsimd.tensor_tensor(out=q[:], in0=live.pop(("praw", b, i))[:], in1=cbc[:, 2, :], op=ALU.add)
+            live[("q", b, i)] = q
+
+        def fin(b, i):
+            if not ok(b):
+                return
+            rstd = st.tile([P, 1], F32, name="rstd", tag="rstd", bufs=3)
+            nc.vector.reciprocal(out=rstd[:], in_=live.pop(("sd", b, i))[:])
+            y = live.pop(("y", b, i))
+            nc.vector.scalar_tensor_tensor(out=y[:], in0=y[:], scalar=rstd[:], in1=live.pop(("q", b, i))[:],
+                                           op0=ALU.mult, op1=ALU.add)
+            r0 = b * TB + i * P
+            nc.sync.dma_start(out=out_rows[r0:r0 + P, :], in_=y[:])
+
+        chunks = []
+        for g in range(NG):
+            for c in range(KP):
+                chunks.append((W2, w2c, w2s, c, 512 * g, True))
+        for c in range(NG):
+            for h in range(2):
+                chunks.append((Wo, woc, wos, c, 512 * h, False))
+        copied = set()
+        wnext = [W_AHEAD]
+
+        def w_load(n):
+            if n >= len(chunks):
+                return
+            src, cod, sca, c, c0, perm = chunks[n]
+            t = wst.tile([P, 4, 512], BF16, name="wraw", tag="wraw", bufs=W_AHEAD)
+            nc.sync.dma_start(out=t[:], in_=src[512 * c:512 * (c + 1), c0:c0 + 512].rearrange("(p j) w -> p j w", j=4))
+            live[("wraw", n)] = t
+
+        def w_copy(n):
+            if n >= len(chunks):
+                return
+            src, cod, sca, c, c0, perm = chunks[n]
+            raw = live.pop(("wraw", n))
+            grp = wst.tile([P, 2048], BF16, name="wgrp", tag="wgrp", bufs=4, align_bytes=64)
+            if perm:
+                o = grp[:].rearrange("p (t m j) -> p t m j", t=4, j=4)
+                s = raw[:].rearrange("p j (m t) -> p t m j", t=4)
+            else:
+                o = grp[:].rearrange("p (w j) -> p w j", j=4)
+                s = raw[:].rearrange("p j w -> p w j")
+            if n % 2 == 0 or n in W_ON_VECTOR:
+                nc.vector.tensor_copy(out=o, in_=s)
+            else:
+                nc.scalar.copy(out=o, in_=s)
+            live[("wgrp", n)] = grp
+            copied.add(n)
+            while (wnext[0] - W_AHEAD) in copied:
+                w_load(wnext[0])
+                wnext[0] = wnext[0] + 1
+
+        def w_quant(n):
+            if n < 0:
+                return
+            src, cod, sca, c, c0, perm = chunks[n]
+            nc.vector.quantize_mx(out=cod[:, c, c0:c0 + 512].bitcast(FP8X4), scales=sca[:, c, c0:c0 + 512],
+                                  in_=live.pop(("wgrp", n))[:])
+
+        def step(k):
+            w_copy(2 * k + 1)
+            w_copy(2 * k)
+            w_quant(2 * k - 2)
+            w_quant(2 * k - 1)
+
+        nc.vector.memset(eps[:], EPS)
+        nc.scalar.activation(out=warm[:], in_=eps[:], func=ACT.Sqrt)
+        make_identity(nc, ident[:])
+        nc.vector.memset(ones[:], 1.0)
+        nc.vector.memset(crow[:], 0.0)
+        nc.vector.memset(xdraw[:], 0.0)
+        load_h(0)
+        nc.scalar.dma_start(out=crow[0:1, 0:ED], in_=bo.rearrange("(o n) -> o n", o=1))
+        nc.scalar.dma_start(out=crow[0:1, ED:2 * ED], in_=ln_out_g.rearrange("(o n) -> o n", o=1))
+        nc.scalar.dma_start(out=crow[0:1, 2 * ED:3 * ED], in_=ln_out_b.rearrange("(o n) -> o n", o=1))
+        nc.scalar.dma_start(out=b2raw[:], in_=b2.rearrange("(g p t) -> p g t", g=NG, t=4))
+        nc.scalar.dma_start(out=xdraw[0:NODES, :], in_=xd_rows)
+        for n in range(W_AHEAD):
+            w_load(n)
+
+        for v in range(3):
+            for h in range(2):
+                pt = bank("cb")
+                nc.tensor.matmul(out=pt[:], lhsT=ones[:], rhs=crow[:, v * ED + h * 512:v * ED + (h + 1) * 512],
+                                 start=True, stop=True)
+                if h == 0:
+                    nc.vector.tensor_copy(out=cbc[:, v, h * 512:(h + 1) * 512], in_=pt[:])
+                else:
+                    nc.scalar.copy(out=cbc[:, v, h * 512:(h + 1) * 512], in_=pt[:])
+        nc.vector.tensor_copy(out=b2f[:], in_=b2raw[:].rearrange("p g t -> p (g t)"))
+        nc.vector.tensor_scalar(out=negb2[:], in0=b2f[:], scalar1=-1.0, scalar2=None, op0=ALU.mult)
+        xt = bank("xt")
+        xw = xdraw[:].bitcast(F32)
+        for u in range(2):
+            nc.tensor.transpose(xt[:, u * P:(u + 1) * P], xw[:, u:256:2], ident[:])
+        xv = xt[:, 0:2 * P].bitcast(BF16).rearrange("p (u n e) -> p u n e", u=2, e=2)
+        for u in range(2):
+            for e in range(2):
+                t = 2 * u + e
+                nc.scalar.activation(out=xi[:, t, :], in_=xv[:, u, 0:NODES, e], func=ACT.Identity,
+                                     bias=b2f[:, t:t + 1], scale=1.0)
+                nc.scalar.activation(out=xj[:, t, 0:NODES], in_=xv[:, u, 0:NODES, e],
+                                     func=ACT.Identity, bias=b2f[:, 4 + t:5 + t], scale=1.0)
+        nc.gpsimd.tensor_copy(out=xj[:, :, NODES:2 * NODES], in_=xj[:, :, 0:NODES])
+        nc.gpsimd.tensor_copy(out=xj[:, :, 2 * NODES:4 * NODES], in_=xj[:, :, 0:2 * NODES])
+        nc.gpsimd.tensor_copy(out=xj[:, :, 4 * NODES:4 * NODES + 16], in_=xj[:, :, 0:16])
+
+        tr1(0)
+        tr_bank(0, "hraw", 3)
+        for c in range(4):
+            cp(0, c)
+        step(0)
+        for c in range(4):
+            qh(0, c)
+        step(1)
+        load_p(0)
+        step(2)
+        m1(0, 0)
+        tr_bank(0, "praw", 0)
+        tr_bank(0, "praw", 1)
+        step(3)
+        load_h(1)
+        xp(0)
+        stt(0, 0, 0)
+        stt(0, 0, 1)
+        step(4)
+        il(0, 0)
+        m1(0, 1)
+        tr1(1)
+        step(5)
+        qs(0, 0)
+        cp(1, 0)
+        cp(1, 1)
+        cp(1, 2)
+        stt(0, 1, 0)
+        stt(0, 1, 1)
+        step(6)
+        load_p(1)
+        il(0, 1)
+        m1(0, 2)
+        tr2(1)
+        qh(1, 0)
+        qh(1, 1)
+        qh(1, 2)
+        step(7)
+        qs(0, 1)
+        cp(1, 3)
+        stt(0, 2, 0)
+        stt(0, 2, 1)
+        step(8)
+        load_h(2)
+        il(0, 2)
+        m1(0, 3)
+        qh(1, 3)
+        xp(1)
+        qs(0, 2)
+        stt(0, 3, 0)
+
+        load_h(3)
+        load_p(2)
+        tr1(2)
+        stt(0, 3, 1)
+        il(0, 3)
+        m1(1, 0)
+        step(9)
+        cp(2, 0)
+        qs(0, 3)
+        cp(2, 1)
+        cp(2, 2)
+        stt(1, 0, 0)
+        m1(1, 1)
+        stt(1, 0, 1)
+        il(1, 0)
+        step(10)
+        qh(2, 0)
+        qh(2, 1)
+        qh(2, 2)
+        stt(1, 1, 0)
+        tr2(2)
+        stt(1, 1, 1)
+        il(1, 1)
+        qs(1, 0)
+        step(11)
+        cp(2, 3)
+        m1(1, 2)
+        qs(1, 1)
+        qadd(0, 0)
+        xp(2)
+        qh(2, 3)
+        stt(1, 2, 0)
+        step(12)
+        m1(1, 3)
+        qadd(0, 1)
+        stt(1, 2, 1)
+        il(1, 2)
+        m2(0, 0)
+        stt(1, 3, 0)
+        qs(1, 2)
+        m2(0, 1)
+        i1(0, 0, 0)
+        i1(0, 0, 1)
+        negmu(0, 0)
+        i3(0, 0)
+        sq(0, 0)
+        i1(0, 1, 0)
+        i1(0, 1, 1)
+        negmu(0, 1)
+        fin(0, 0)
+        i3(0, 1)
+        sq(0, 1)
+
+        for b in range(2, NB + 2):
+            load_h(b + 2)
+            load_p(b + 1)
+            tr1(b + 1)
+            stt(b - 1, 3, 1)
+            cp(b + 1, 0)
+            fin(b - 2, 1)
+            il(b - 1, 3)
+            m1(b, 0)
+            qadd(b - 1, 0)
+            cp(b + 1, 1)
+            cp(b + 1, 2)
+            qs(b - 1, 3)
+            stt(b, 0, 0)
+            qh(b + 1, 0)
+            qh(b + 1, 1)
+            qh(b + 1, 2)
+            m1(b, 1)
+            stt(b, 0, 1)
+            il(b, 0)
+            stt(b, 1, 0)
+            m2(b - 1, 0)
+            stt(b, 1, 1)
+            il(b, 1)
+            qs(b, 0)
+            i1(b - 1, 0, 0)
+            qs(b, 1)
+            tr2(b + 1)
+            i1(b - 1, 0, 1)
+            negmu(b - 1, 0)
+            cp(b + 1, 3)
+            i3(b - 1, 0)
+            sq(b - 1, 0)
+            m1(b, 2)
+            qh(b + 1, 3)
+            fin(b - 1, 0)
+            xp(b + 1)
+            stt(b, 2, 0)
+            qadd(b - 1, 1)
+            m2(b - 1, 1)
+            stt(b, 2, 1)
+            il(b, 2)
+            i1(b - 1, 1, 0)
+            qs(b, 2)
+            m1(b, 3)
+            i1(b - 1, 1, 1)
+            negmu(b - 1, 1)
+            i3(b - 1, 1)
+            sq(b - 1, 1)
+            stt(b, 3, 0)

@@ -22,7 +22,8 @@ TB = 256
 NB = TOKENS // TB
 KP = 4
 NG = 4
-W_AHEAD = 5
+W_AHEAD = 6
+F4K = 11
 W_ON_VECTOR = ()
 
 FLOPS = 2 * TOKENS * F_IN * MD + 2 * TOKENS * MD * ED
@@ -37,7 +38,6 @@ def tile_edgeupdaterwrapper_v01_pb_l_kernel(tc, hid, x_down, p_ln, W2, b2, Wo, b
 
     with ExitStack() as ctx:
         keep = ctx.enter_context(tc.tile_pool(name="keep", bufs=1))
-        wst = ctx.enter_context(tc.tile_pool(name="wst", bufs=3))
         st = ctx.enter_context(tc.tile_pool(name="st", bufs=2))
         psum = ctx.enter_context(tc.psum_pool(name="psum", bufs=8))
         ctx.enter_context(tc.manual_schedule())
@@ -184,6 +184,32 @@ def tile_edgeupdaterwrapper_v01_pb_l_kernel(tc, hid, x_down, p_ln, W2, b2, Wo, b
                     nc.vector.scalar_tensor_tensor(out=sp[:, t, :], in0=pt[:, h * TB:(h + 1) * TB],
                                                    scalar=negb2[:, col:col + 1], in1=x, op0=ALU.max, op1=ALU.add)
 
+        def g0r(b, k):
+            if not ok(b):
+                return
+            if k == 0:
+                live[("r0", b)] = st.tile([P, 4, TB], F32, name="r0", tag="f4k", bufs=F4K, align_bytes=64)
+            pt = live.pop(("s1", b, 0, k))
+            for h in range(2):
+                t = 2 * k + h
+                nc.scalar.activation(out=live[("r0", b)][:, t, :], in_=pt[:, h * TB:(h + 1) * TB], func=ACT.Relu,
+                                     bias=b2f[:, t:t + 1], scale=1.0)
+
+        def g0a(b):
+            if not ok(b):
+                return
+            sp = st.tile([P, 4, TB], BF16, name="sp", tag="sp", bufs=3)
+            r0 = live.pop(("r0", b))
+            for t in range(4):
+                lo = 0
+                while lo < TB:
+                    i = (b * TB + lo) // NODES
+                    hi = min(TB, (i + 1) * NODES - b * TB)
+                    nc.scalar.activation(out=sp[:, t, lo:hi], in_=r0[:, t, lo:hi], func=ACT.Identity,
+                                         bias=xi[:, t, i:i + 1], scale=1.0)
+                    lo = hi
+            live[("sp", b, 0)] = sp
+
         def il(b, g):
             if not ok(b):
                 return
@@ -221,7 +247,7 @@ def tile_edgeupdaterwrapper_v01_pb_l_kernel(tc, hid, x_down, p_ln, W2, b2, Wo, b
             if not ok(b):
                 return
             if h == 0:
-                live[("z", b, i)] = st.tile([P, ED], F32, name="z", tag="z", bufs=2)
+                live[("z", b, i)] = st.tile([P, ED], F32, name="z", tag="f4k", bufs=F4K, align_bytes=64)
                 live[("zs", b, i)] = st.tile([P, 2], F32, name="zs", tag="zs", bufs=3)
             pt = live.pop(("s2", b, i, h))
             nc.vector.scalar_tensor_tensor(out=live[("z", b, i)][:, h * 512:(h + 1) * 512], in0=pt[:], scalar=1.0,
@@ -233,14 +259,14 @@ def tile_edgeupdaterwrapper_v01_pb_l_kernel(tc, hid, x_down, p_ln, W2, b2, Wo, b
                 return
             nm = st.tile([P, 1], F32, name="nm", tag="nm", bufs=3)
             zs = live.pop(("zs", b, i))
-            nc.vector.tensor_scalar(out=nm[:], in0=zs[:, 0:1], scalar1=zs[:, 1:2], scalar2=-1.0 / ED,
-                                    op0=ALU.add, op1=ALU.mult)
+            zj = st.tile([P, 2], F32, name="zj", tag="zj", bufs=2)
+            nc.scalar.activation(out=zj[:], in_=zs[:], func=ACT.Identity, scale=-1.0 / ED, accum_out=nm[:])
             live[("nm", b, i)] = nm
 
         def i3(b, i):
             if not ok(b):
                 return
-            y = st.tile([P, ED], F32, name="y", tag="y", bufs=3)
+            y = st.tile([P, ED], F32, name="y", tag="f4k", bufs=F4K, align_bytes=64)
             nc.vector.scalar_tensor_tensor(out=y[:], in0=live[("z", b, i)][:], scalar=live[("nm", b, i)][:],
                                            in1=cbc[:, 1, :], op0=ALU.add, op1=ALU.mult)
             live[("y", b, i)] = y
@@ -251,23 +277,35 @@ def tile_edgeupdaterwrapper_v01_pb_l_kernel(tc, hid, x_down, p_ln, W2, b2, Wo, b
             junk = st.tile([P, ED], BF16, name="junk", tag="junk", bufs=1)
             ssq = st.tile([P, 1], F32, name="ssq", tag="ssq", bufs=3)
             sd = st.tile([P, 1], F32, name="sd", tag="sd", bufs=3)
-            nc.scalar.activation(out=junk[:], in_=live.pop(("z", b, i))[:], func=ACT.Square,
-                                 bias=live.pop(("nm", b, i))[:], scale=1.0, accum_out=ssq[:])
-            nc.scalar.activation(out=sd[:], in_=ssq[:], func=ACT.Sqrt, bias=eps[:], scale=1.0 / ED)
+            nc.scalar.activation(out=junk[:], in_=live[("z", b, i)][:], func=ACT.Square,
+                                 bias=live[("nm", b, i)][:], scale=1.0, accum_out=ssq[:])
+            live[("ssq", b, i)] = ssq
             live[("sd", b, i)] = sd
+
+        def sqr(b, i):
+            if not ok(b):
+                return
+            nc.scalar.activation(out=live[("sd", b, i)][:], in_=live.pop(("ssq", b, i))[:], func=ACT.Sqrt, bias=eps[:],
+                                 scale=1.0 / ED)
 
         def qadd(b, i):
             if not ok(b):
                 return
-            q = st.tile([P, ED], F32, name="q", tag="q", bufs=2)
-            nc.gpsimd.tensor_tensor(out=q[:], in0=live.pop(("praw", b, i))[:], in1=cbc[:, 2, :], op=ALU.add)
+            q = st.tile([P, ED], F32, name="q", tag="f4k", bufs=F4K, align_bytes=64)
+            nc.vector.tensor_tensor(out=q[:], in0=live.pop(("praw", b, i))[:], in1=cbc[:, 2, :], op=ALU.add)
             live[("q", b, i)] = q
 
-        def fin(b, i):
+        def rcp(b, i):
             if not ok(b):
                 return
             rstd = st.tile([P, 1], F32, name="rstd", tag="rstd", bufs=3)
             nc.vector.reciprocal(out=rstd[:], in_=live.pop(("sd", b, i))[:])
+            live[("rstd", b, i)] = rstd
+
+        def fin(b, i):
+            if not ok(b):
+                return
+            rstd = live.pop(("rstd", b, i))
             y = live.pop(("y", b, i))
             nc.vector.scalar_tensor_tensor(out=y[:], in0=y[:], scalar=rstd[:], in1=live.pop(("q", b, i))[:],
                                            op0=ALU.mult, op1=ALU.add)
@@ -288,7 +326,7 @@ def tile_edgeupdaterwrapper_v01_pb_l_kernel(tc, hid, x_down, p_ln, W2, b2, Wo, b
             if n >= len(chunks):
                 return
             src, cod, sca, c, c0, perm = chunks[n]
-            t = wst.tile([P, 4, 512], BF16, name="wraw", tag="wraw", bufs=W_AHEAD)
+            t = st.tile([P, 4, 512], BF16, name="wraw", tag="f4k", bufs=F4K, align_bytes=64)
             nc.sync.dma_start(out=t[:], in_=src[512 * c:512 * (c + 1), c0:c0 + 512].rearrange("(p j) w -> p j w", j=4))
             live[("wraw", n)] = t
 
@@ -297,7 +335,7 @@ def tile_edgeupdaterwrapper_v01_pb_l_kernel(tc, hid, x_down, p_ln, W2, b2, Wo, b
                 return
             src, cod, sca, c, c0, perm = chunks[n]
             raw = live.pop(("wraw", n))
-            grp = wst.tile([P, 2048], BF16, name="wgrp", tag="wgrp", bufs=4, align_bytes=64)
+            grp = st.tile([P, 2048], BF16, name="wgrp", tag="f4k", bufs=F4K, align_bytes=64)
             if perm:
                 o = grp[:].rearrange("p (t m j) -> p t m j", t=4, j=4)
                 s = raw[:].rearrange("p j (m t) -> p t m j", t=4)
@@ -361,8 +399,7 @@ def tile_edgeupdaterwrapper_v01_pb_l_kernel(tc, hid, x_down, p_ln, W2, b2, Wo, b
         for u in range(2):
             for e in range(2):
                 t = 2 * u + e
-                nc.scalar.activation(out=xi[:, t, :], in_=xv[:, u, 0:NODES, e], func=ACT.Identity,
-                                     bias=b2f[:, t:t + 1], scale=1.0)
+                nc.scalar.copy(out=xi[:, t, :], in_=xv[:, u, 0:NODES, e])
                 nc.scalar.activation(out=xj[:, t, 0:NODES], in_=xv[:, u, 0:NODES, e],
                                      func=ACT.Identity, bias=b2f[:, 4 + t:5 + t], scale=1.0)
         nc.gpsimd.tensor_copy(out=xj[:, :, NODES:2 * NODES], in_=xj[:, :, 0:NODES])
@@ -384,10 +421,11 @@ def tile_edgeupdaterwrapper_v01_pb_l_kernel(tc, hid, x_down, p_ln, W2, b2, Wo, b
         tr_bank(0, "praw", 1)
         step(3)
         load_h(1)
+        g0r(0, 0)
+        g0r(0, 1)
         xp(0)
-        stt(0, 0, 0)
-        stt(0, 0, 1)
         step(4)
+        g0a(0)
         il(0, 0)
         m1(0, 1)
         tr1(1)
@@ -431,9 +469,10 @@ def tile_edgeupdaterwrapper_v01_pb_l_kernel(tc, hid, x_down, p_ln, W2, b2, Wo, b
         qs(0, 3)
         cp(2, 1)
         cp(2, 2)
-        stt(1, 0, 0)
+        g0r(1, 0)
         m1(1, 1)
-        stt(1, 0, 1)
+        g0r(1, 1)
+        g0a(1)
         il(1, 0)
         step(10)
         qh(2, 0)
@@ -448,78 +487,85 @@ def tile_edgeupdaterwrapper_v01_pb_l_kernel(tc, hid, x_down, p_ln, W2, b2, Wo, b
         cp(2, 3)
         m1(1, 2)
         qs(1, 1)
-        qadd(0, 0)
         xp(2)
         qh(2, 3)
         stt(1, 2, 0)
         step(12)
         m1(1, 3)
-        qadd(0, 1)
         stt(1, 2, 1)
         il(1, 2)
         m2(0, 0)
-        stt(1, 3, 0)
+        qadd(0, 0)
         qs(1, 2)
         m2(0, 1)
         i1(0, 0, 0)
         i1(0, 0, 1)
         negmu(0, 0)
-        i3(0, 0)
+        qadd(0, 1)
         sq(0, 0)
+        sqr(0, 0)
+        i3(0, 0)
         i1(0, 1, 0)
+        rcp(0, 0)
         i1(0, 1, 1)
         negmu(0, 1)
         fin(0, 0)
-        i3(0, 1)
         sq(0, 1)
+        stt(1, 3, 0)
+        i3(0, 1)
 
         for b in range(2, NB + 2):
             load_h(b + 2)
             load_p(b + 1)
             tr1(b + 1)
             stt(b - 1, 3, 1)
+            sqr(b - 2, 1)
+            rcp(b - 2, 1)
             cp(b + 1, 0)
-            fin(b - 2, 1)
+            qadd(b - 1, 0)
             il(b - 1, 3)
             m1(b, 0)
-            qadd(b - 1, 0)
+            fin(b - 2, 1)
             cp(b + 1, 1)
-            cp(b + 1, 2)
             qs(b - 1, 3)
-            stt(b, 0, 0)
+            g0r(b, 0)
             qh(b + 1, 0)
             qh(b + 1, 1)
-            qh(b + 1, 2)
+            cp(b + 1, 2)
+            qadd(b - 1, 1)
             m1(b, 1)
-            stt(b, 0, 1)
-            il(b, 0)
+            g0r(b, 1)
+            qh(b + 1, 2)
+            g0a(b)
             stt(b, 1, 0)
             m2(b - 1, 0)
             stt(b, 1, 1)
+            il(b, 0)
+            i1(b - 1, 0, 0)
             il(b, 1)
             qs(b, 0)
-            i1(b - 1, 0, 0)
-            qs(b, 1)
             tr2(b + 1)
             i1(b - 1, 0, 1)
+            qs(b, 1)
             negmu(b - 1, 0)
             cp(b + 1, 3)
             i3(b - 1, 0)
             sq(b - 1, 0)
+            sqr(b - 1, 0)
             m1(b, 2)
             qh(b + 1, 3)
-            fin(b - 1, 0)
             xp(b + 1)
             stt(b, 2, 0)
-            qadd(b - 1, 1)
+            rcp(b - 1, 0)
             m2(b - 1, 1)
             stt(b, 2, 1)
+            fin(b - 1, 0)
             il(b, 2)
             i1(b - 1, 1, 0)
-            qs(b, 2)
             m1(b, 3)
             i1(b - 1, 1, 1)
+            qs(b, 2)
             negmu(b - 1, 1)
-            i3(b - 1, 1)
             sq(b - 1, 1)
             stt(b, 3, 0)
+            i3(b - 1, 1)

@@ -24,7 +24,11 @@ KP = 4
 NG = 4
 W_AHEAD = 6
 F4K = 11
-W_ON_VECTOR = ()
+W_ON_VECTOR = (3, 11, 17, 19, 21, 23)
+POSTPONED = 2
+SORT_FROM = 4
+FIRST_LATE = 3
+LATE_EVERY = 2
 
 FLOPS = 2 * TOKENS * F_IN * MD + 2 * TOKENS * MD * ED
 
@@ -48,7 +52,6 @@ def tile_edgeupdaterwrapper_v01_pb_l_kernel(tc, hid, x_down, p_ln, W2, b2, Wo, b
         wos = keep.tile([P, NG, ED], U8, name="wos", align_bytes=64)
         ident = keep.tile([P, P], F32, name="ident")
         ones = keep.tile([P, P], BF16, name="ones")
-        crow = keep.tile([P, 3 * ED], BF16, name="crow")
         cbc = keep.tile([P, 3, ED], BF16, name="cbc")
         b2raw = keep.tile([P, NG, 4], BF16, name="b2raw")
         b2f = keep.tile([P, NG * 4], F32, name="b2f")
@@ -80,18 +83,28 @@ def tile_edgeupdaterwrapper_v01_pb_l_kernel(tc, hid, x_down, p_ln, W2, b2, Wo, b
             if not ok(b):
                 return
             for i in range(2):
-                t = st.tile([P, ED], BF16, name="praw", tag="praw", bufs=6)
+                t = st.tile([P, ED], BF16, name="praw", tag="praw", bufs=12)
                 r0 = b * TB + i * P
                 nc.sync.dma_start(out=t[:], in_=pln_rows[r0:r0 + P, :])
                 live[("praw", b, i)] = t
+
+        def srt_p(b, i):
+            if not ok(b) or b < SORT_FROM:
+                return
+            t = st.tile([P, ED], BF16, name="psrt", tag="psrt", bufs=2)
+            nc.vector.tensor_copy(out=t[:].bitcast(F32).rearrange("p (c u m) -> p c u m", c=2, u=2),
+                                  in_=live[("praw", b, i)][:].bitcast(F32).rearrange("p (c m u) -> p c u m", c=2, u=2))
+            live[("psrt", b, i)] = t
 
         def tr_bank(b, kind, c):
             pt = bank("tp")
             for u in range(2):
                 for i in range(2):
-                    words = live[(kind, b, i)][:].bitcast(F32)
-                    nc.tensor.transpose(pt[:, u * TB + i * P:u * TB + (i + 1) * P],
-                                        words[:, 256 * c + u:256 * (c + 1):2], ident[:])
+                    if kind == "praw" and b >= SORT_FROM:
+                        words = live[("psrt", b, i)][:].bitcast(F32)[:, 256 * c + P * u:256 * c + P * (u + 1)]
+                    else:
+                        words = live[(kind, b, i)][:].bitcast(F32)[:, 256 * c + u:256 * (c + 1):2]
+                    nc.tensor.transpose(pt[:, u * TB + i * P:u * TB + (i + 1) * P], words, ident[:])
             live[("tp", kind, b, c)] = pt
 
         def tr1(b):
@@ -222,8 +235,8 @@ def tile_edgeupdaterwrapper_v01_pb_l_kernel(tc, hid, x_down, p_ln, W2, b2, Wo, b
             if not ok(b):
                 return
             if g == 0:
-                live[("sc", b)] = st.tile([P, NG, TB], U32, name="sc", tag="sc", bufs=2, align_bytes=64)
-                live[("ss", b)] = st.tile([P, NG, TB], U8, name="ss", tag="ss", bufs=2, align_bytes=64)
+                live[("sc", b)] = st.tile([P, NG, TB], U32, name="sc", tag="sc", bufs=4, align_bytes=64)
+                live[("ss", b)] = st.tile([P, NG, TB], U8, name="ss", tag="ss", bufs=4, align_bytes=64)
             sg = live.pop(("sg", b, g))
             nc.vector.quantize_mx(out=live[("sc", b)][:, g, :].bitcast(FP8X4), scales=live[("ss", b)][:, g, :],
                                   in_=sg[:].rearrange("p n t -> p (n t)"))
@@ -289,7 +302,7 @@ def tile_edgeupdaterwrapper_v01_pb_l_kernel(tc, hid, x_down, p_ln, W2, b2, Wo, b
                                  scale=1.0 / ED)
 
         def qadd(b, i):
-            if not ok(b):
+            if not ok(b) or ("q", b, i) in live:
                 return
             q = st.tile([P, ED], F32, name="q", tag="f4k", bufs=F4K, align_bytes=64)
             nc.vector.tensor_tensor(out=q[:], in0=live.pop(("praw", b, i))[:], in1=cbc[:, 2, :], op=ALU.add)
@@ -365,25 +378,28 @@ def tile_edgeupdaterwrapper_v01_pb_l_kernel(tc, hid, x_down, p_ln, W2, b2, Wo, b
             w_quant(2 * k - 2)
             w_quant(2 * k - 1)
 
-        nc.vector.memset(eps[:], EPS)
-        nc.scalar.activation(out=warm[:], in_=eps[:], func=ACT.Sqrt)
-        make_identity(nc, ident[:])
-        nc.vector.memset(ones[:], 1.0)
-        nc.vector.memset(crow[:], 0.0)
-        nc.vector.memset(xdraw[:], 0.0)
         load_h(0)
-        nc.scalar.dma_start(out=crow[0:1, 0:ED], in_=bo.rearrange("(o n) -> o n", o=1))
-        nc.scalar.dma_start(out=crow[0:1, ED:2 * ED], in_=ln_out_g.rearrange("(o n) -> o n", o=1))
-        nc.scalar.dma_start(out=crow[0:1, 2 * ED:3 * ED], in_=ln_out_b.rearrange("(o n) -> o n", o=1))
-        nc.scalar.dma_start(out=b2raw[:], in_=b2.rearrange("(g p t) -> p g t", g=NG, t=4))
-        nc.scalar.dma_start(out=xdraw[0:NODES, :], in_=xd_rows)
+        crow = []
+        for v in range(3):
+            crow.append(st.tile([P, ED], BF16, name="crow", tag="sp", bufs=3))
+            nc.vector.memset(crow[v][:], 0.0)
+        nc.gpsimd.memset(xdraw[:], 0.0)
+        nc.vector.memset(eps[:], EPS)
+        nc.vector.memset(ones[:], 1.0)
+        make_identity(nc, ident[:])
+        nc.scalar.activation(out=warm[:], in_=eps[:], func=ACT.Sqrt)
+        nc.sync.dma_start(out=b2raw[:], in_=b2.rearrange("(g p t) -> p g t", g=NG, t=4))
+        nc.sync.dma_start(out=xdraw[0:NODES, :], in_=xd_rows)
+        nc.sync.dma_start(out=crow[0][0:1, :], in_=bo.rearrange("(o n) -> o n", o=1))
+        nc.sync.dma_start(out=crow[1][0:1, :], in_=ln_out_g.rearrange("(o n) -> o n", o=1))
+        nc.sync.dma_start(out=crow[2][0:1, :], in_=ln_out_b.rearrange("(o n) -> o n", o=1))
         for n in range(W_AHEAD):
             w_load(n)
 
         for v in range(3):
             for h in range(2):
                 pt = bank("cb")
-                nc.tensor.matmul(out=pt[:], lhsT=ones[:], rhs=crow[:, v * ED + h * 512:v * ED + (h + 1) * 512],
+                nc.tensor.matmul(out=pt[:], lhsT=ones[:], rhs=crow[v][:, h * 512:(h + 1) * 512],
                                  start=True, stop=True)
                 if h == 0:
                     nc.vector.tensor_copy(out=cbc[:, v, h * 512:(h + 1) * 512], in_=pt[:])
@@ -451,6 +467,7 @@ def tile_edgeupdaterwrapper_v01_pb_l_kernel(tc, hid, x_down, p_ln, W2, b2, Wo, b
         stt(0, 2, 1)
         step(8)
         load_h(2)
+        load_p(2)
         il(0, 2)
         m1(0, 3)
         qh(1, 3)
@@ -458,114 +475,130 @@ def tile_edgeupdaterwrapper_v01_pb_l_kernel(tc, hid, x_down, p_ln, W2, b2, Wo, b
         qs(0, 2)
         stt(0, 3, 0)
 
-        load_h(3)
-        load_p(2)
-        tr1(2)
-        stt(0, 3, 1)
-        il(0, 3)
-        m1(1, 0)
-        step(9)
-        cp(2, 0)
-        qs(0, 3)
-        cp(2, 1)
-        cp(2, 2)
-        g0r(1, 0)
-        m1(1, 1)
-        g0r(1, 1)
-        g0a(1)
-        il(1, 0)
-        step(10)
-        qh(2, 0)
-        qh(2, 1)
-        qh(2, 2)
-        stt(1, 1, 0)
-        tr2(2)
-        stt(1, 1, 1)
-        il(1, 1)
-        qs(1, 0)
-        step(11)
-        cp(2, 3)
-        m1(1, 2)
-        qs(1, 1)
-        xp(2)
-        qh(2, 3)
-        stt(1, 2, 0)
-        step(12)
-        m1(1, 3)
-        stt(1, 2, 1)
-        il(1, 2)
-        m2(0, 0)
-        qadd(0, 0)
-        qs(1, 2)
-        m2(0, 1)
-        i1(0, 0, 0)
-        i1(0, 0, 1)
-        negmu(0, 0)
-        qadd(0, 1)
-        sq(0, 0)
-        sqr(0, 0)
-        i3(0, 0)
-        i1(0, 1, 0)
-        rcp(0, 0)
-        i1(0, 1, 1)
-        negmu(0, 1)
-        fin(0, 0)
-        sq(0, 1)
-        stt(1, 3, 0)
-        i3(0, 1)
+        def late(b):
+            k = b - FIRST_LATE
+            if k % LATE_EVERY == 0 and 0 <= k // LATE_EVERY < 2 * POSTPONED:
+                return (k // LATE_EVERY // 2, k // LATE_EVERY % 2)
+            return (-1, 0)
 
-        for b in range(2, NB + 2):
+        for b in range(1, NB):
+            c = b - 1 if b - 1 >= POSTPONED else -1
+            d = b - 2 if b - 2 >= POSTPONED else -1
+            eb, ei = late(b)
+            fb, fi = late(b - 1)
             load_h(b + 2)
-            load_p(b + 1)
+            load_p(b + 2)
             tr1(b + 1)
             stt(b - 1, 3, 1)
-            sqr(b - 2, 1)
-            rcp(b - 2, 1)
+            sqr(d, 1)
+            rcp(d, 1)
             cp(b + 1, 0)
-            qadd(b - 1, 0)
+            i1(fb, fi, 0)
+            qadd(c, 0)
             il(b - 1, 3)
             m1(b, 0)
-            fin(b - 2, 1)
+            i1(fb, fi, 1)
+            negmu(fb, fi)
+            fin(d, 1)
             cp(b + 1, 1)
+            sq(fb, fi)
+            sqr(fb, fi)
             qs(b - 1, 3)
+            srt_p(b + 1, 0)
+            srt_p(b + 1, 1)
             g0r(b, 0)
+            if b == 1:
+                step(9)
+            if b == 2:
+                step(11)
             qh(b + 1, 0)
             qh(b + 1, 1)
             cp(b + 1, 2)
-            qadd(b - 1, 1)
+            i3(fb, fi)
+            qadd(c, 1)
             m1(b, 1)
             g0r(b, 1)
             qh(b + 1, 2)
+            rcp(fb, fi)
             g0a(b)
             stt(b, 1, 0)
-            m2(b - 1, 0)
+            m2(c, 0)
+            fin(fb, fi)
             stt(b, 1, 1)
             il(b, 0)
-            i1(b - 1, 0, 0)
+            i1(c, 0, 0)
             il(b, 1)
             qs(b, 0)
             tr2(b + 1)
-            i1(b - 1, 0, 1)
+            i1(c, 0, 1)
             qs(b, 1)
-            negmu(b - 1, 0)
+            negmu(c, 0)
             cp(b + 1, 3)
-            i3(b - 1, 0)
-            sq(b - 1, 0)
-            sqr(b - 1, 0)
+            i3(c, 0)
+            sq(c, 0)
+            sqr(c, 0)
             m1(b, 2)
+            if b == 1:
+                step(10)
+            if b == 2:
+                step(12)
             qh(b + 1, 3)
             xp(b + 1)
             stt(b, 2, 0)
-            rcp(b - 1, 0)
-            m2(b - 1, 1)
-            stt(b, 2, 1)
-            fin(b - 1, 0)
-            il(b, 2)
-            i1(b - 1, 1, 0)
-            m1(b, 3)
-            i1(b - 1, 1, 1)
-            qs(b, 2)
-            negmu(b - 1, 1)
-            sq(b - 1, 1)
-            stt(b, 3, 0)
-            i3(b - 1, 1)
+            rcp(c, 0)
+            if b == NB - 1:
+                m1(b, 3)
+                stt(b, 2, 1)
+                fin(c, 0)
+                il(b, 2)
+                m2(c, 1)
+                stt(b, 3, 0)
+                qs(b, 2)
+                stt(b, 3, 1)
+                il(b, 3)
+                i1(c, 1, 0)
+                qadd(b, 0)
+                i1(c, 1, 1)
+                qs(b, 3)
+                negmu(c, 1)
+                sq(c, 1)
+                qadd(b, 1)
+                i3(c, 1)
+            else:
+                m2(c, 1)
+                stt(b, 2, 1)
+                fin(c, 0)
+                il(b, 2)
+                i1(c, 1, 0)
+                m1(b, 3)
+                m2(eb, ei)
+                i1(c, 1, 1)
+                qs(b, 2)
+                negmu(c, 1)
+                sq(c, 1)
+                stt(b, 3, 0)
+                qadd(eb, ei)
+                i3(c, 1)
+
+        c = NB - 1
+        sqr(c - 1, 1)
+        rcp(c - 1, 1)
+        m2(c, 0)
+        m2(c, 1)
+        fin(c - 1, 1)
+        i1(c, 0, 0)
+        i1(c, 0, 1)
+        negmu(c, 0)
+        i1(c, 1, 0)
+        sq(c, 0)
+        sqr(c, 0)
+        i1(c, 1, 1)
+        negmu(c, 1)
+        i3(c, 0)
+        sq(c, 1)
+        sqr(c, 1)
+        rcp(c, 0)
+        i3(c, 1)
+        rcp(c, 1)
+        fin(c, 0)
+        fin(c, 1)

@@ -26,7 +26,6 @@ W_AHEAD = 6
 F4K = 11
 W_ON_VECTOR = (3, 11, 17, 19, 21, 23)
 POSTPONED = 2
-SORT_FROM = 4
 FIRST_LATE = 3
 LATE_EVERY = 2
 
@@ -83,28 +82,18 @@ def tile_edgeupdaterwrapper_v01_pb_l_kernel(tc, hid, x_down, p_ln, W2, b2, Wo, b
             if not ok(b):
                 return
             for i in range(2):
-                t = st.tile([P, ED], BF16, name="praw", tag="praw", bufs=12)
+                t = st.tile([P, ED], BF16, name="praw", tag="praw", bufs=10)
                 r0 = b * TB + i * P
                 nc.sync.dma_start(out=t[:], in_=pln_rows[r0:r0 + P, :])
                 live[("praw", b, i)] = t
-
-        def srt_p(b, i):
-            if not ok(b) or b < SORT_FROM:
-                return
-            t = st.tile([P, ED], BF16, name="psrt", tag="psrt", bufs=2)
-            nc.vector.tensor_copy(out=t[:].bitcast(F32).rearrange("p (c u m) -> p c u m", c=2, u=2),
-                                  in_=live[("praw", b, i)][:].bitcast(F32).rearrange("p (c m u) -> p c u m", c=2, u=2))
-            live[("psrt", b, i)] = t
 
         def tr_bank(b, kind, c):
             pt = bank("tp")
             for u in range(2):
                 for i in range(2):
-                    if kind == "praw" and b >= SORT_FROM:
-                        words = live[("psrt", b, i)][:].bitcast(F32)[:, 256 * c + P * u:256 * c + P * (u + 1)]
-                    else:
-                        words = live[(kind, b, i)][:].bitcast(F32)[:, 256 * c + u:256 * (c + 1):2]
-                    nc.tensor.transpose(pt[:, u * TB + i * P:u * TB + (i + 1) * P], words, ident[:])
+                    words = live[(kind, b, i)][:].bitcast(F32)
+                    nc.tensor.transpose(pt[:, u * TB + i * P:u * TB + (i + 1) * P],
+                                        words[:, 256 * c + u:256 * (c + 1):2], ident[:])
             live[("tp", kind, b, c)] = pt
 
         def tr1(b):
@@ -467,7 +456,6 @@ def tile_edgeupdaterwrapper_v01_pb_l_kernel(tc, hid, x_down, p_ln, W2, b2, Wo, b
         stt(0, 2, 1)
         step(8)
         load_h(2)
-        load_p(2)
         il(0, 2)
         m1(0, 3)
         qh(1, 3)
@@ -487,7 +475,7 @@ def tile_edgeupdaterwrapper_v01_pb_l_kernel(tc, hid, x_down, p_ln, W2, b2, Wo, b
             eb, ei = late(b)
             fb, fi = late(b - 1)
             load_h(b + 2)
-            load_p(b + 2)
+            load_p(b + 1)
             tr1(b + 1)
             stt(b - 1, 3, 1)
             sqr(d, 1)
@@ -504,8 +492,6 @@ def tile_edgeupdaterwrapper_v01_pb_l_kernel(tc, hid, x_down, p_ln, W2, b2, Wo, b
             sq(fb, fi)
             sqr(fb, fi)
             qs(b - 1, 3)
-            srt_p(b + 1, 0)
-            srt_p(b + 1, 1)
             g0r(b, 0)
             if b == 1:
                 step(9)

from contextlib import ExitStack

import concourse.mybir as mybir
from concourse.masks import make_identity

F32 = mybir.dt.float32
BF16 = mybir.dt.bfloat16
U32 = mybir.dt.uint32
U8 = mybir.dt.uint8
FP8X4 = mybir.dt.float8_e4m3fn_x4
ALU = mybir.AluOpType
ACT = mybir.ActivationFunctionType

P = 128
NODES = 80
TOKENS = NODES * NODES
F_IN = 2048
MD = 2048
ED = 1024
EPS = 1e-5
TB = 256
NB = TOKENS // TB
KP = 4
NG = 4
W_AHEAD = 6
F4K = 11
W_ON_VECTOR = (3, 11, 17, 19, 21, 23)
POSTPONED = 2
FIRST_LATE = 3
LATE_EVERY = 2

FLOPS = 2 * TOKENS * F_IN * MD + 2 * TOKENS * MD * ED


def tile_edgeupdaterwrapper_v01_pb_l_kernel(tc, hid, x_down, p_ln, W2, b2, Wo, bo, ln_out_g, ln_out_b, out):
    nc = tc.nc
    hid_rows = hid.flatten_outer_dims()
    pln_rows = p_ln.flatten_outer_dims()
    out_rows = out.flatten_outer_dims()
    xd_rows = x_down.flatten_outer_dims()

    with ExitStack() as ctx:
        keep = ctx.enter_context(tc.tile_pool(name="keep", bufs=1))
        st = ctx.enter_context(tc.tile_pool(name="st", bufs=2))
        psum = ctx.enter_context(tc.psum_pool(name="psum", bufs=8))
        ctx.enter_context(tc.manual_schedule())

        w2c = keep.tile([P, KP, MD], U32, name="w2c", align_bytes=64)
        w2s = keep.tile([P, KP, MD], U8, name="w2s", align_bytes=64)
        woc = keep.tile([P, NG, ED], U32, name="woc", align_bytes=64)
        wos = keep.tile([P, NG, ED], U8, name="wos", align_bytes=64)
        ident = keep.tile([P, P], F32, name="ident")
        ones = keep.tile([P, P], BF16, name="ones")
        cbc = keep.tile([P, 3, ED], BF16, name="cbc")
        b2raw = keep.tile([P, NG, 4], BF16, name="b2raw")
        b2f = keep.tile([P, NG * 4], F32, name="b2f")
        negb2 = keep.tile([P, NG * 4], F32, name="negb2")
        xdraw = keep.tile([P, 512], BF16, name="xdraw")
        xi = keep.tile([P, 4, NODES], F32, name="xi")
        xj = keep.tile([P, 4, 4 * NODES + 16], F32, name="xj")
        eps = keep.tile([P, 1], F32, name="eps")
        warm = keep.tile([P, 1], F32, name="warm")

        live = {}

        def bank(nm):
            return psum.tile([P, 512], F32, name=nm, tag="bank")

        def ok(b):
            return 0 <= b < NB

        def load_h(b):
            if not ok(b):
                return
            for i in range(2):
                t = st.tile([P, F_IN], BF16, name="hraw", tag="hraw", bufs=4)
                r0 = b * TB + i * P
                nc.sync.dma_start(out=t[:], in_=hid_rows[r0:r0 + P, :])
                live[("hraw", b, i)] = t

        def load_p(b):
            if not ok(b):
                return
            for i in range(2):
                t = st.tile([P, ED], BF16, name="praw", tag="praw", bufs=10)
                r0 = b * TB + i * P
                nc.sync.dma_start(out=t[:], in_=pln_rows[r0:r0 + P, :])
                live[("praw", b, i)] = t

        def tr_bank(b, kind, c):
            pt = bank("tp")
            for u in range(2):
                for i in range(2):
                    words = live[(kind, b, i)][:].bitcast(F32)
                    nc.tensor.transpose(pt[:, u * TB + i * P:u * TB + (i + 1) * P],
                                        words[:, 256 * c + u:256 * (c + 1):2], ident[:])
            live[("tp", kind, b, c)] = pt

        def tr1(b):
            if not ok(b):
                return
            for c in range(3):
                tr_bank(b, "hraw", c)

        def tr2(b):
            if not ok(b):
                return
            tr_bank(b, "hraw", 3)
            tr_bank(b, "praw", 0)
            tr_bank(b, "praw", 1)

        def cp(b, c):
            if not ok(b):
                return
            pt = live.pop(("tp", "hraw", b, c))
            hg = st.tile([P, 4 * TB], BF16, name="hg", tag="hg", bufs=4, align_bytes=64)
            nc.scalar.copy(out=hg[:].bitcast(F32).rearrange("p (n u) -> p n u", u=2),
                           in_=pt[:].rearrange("p (u n) -> p n u", u=2))
            live[("hg", b, c)] = hg

        def qh(b, c):
            if not ok(b):
                return
            if c == 0:
                live[("hc", b)] = st.tile([P, KP, TB], U32, name="hc", tag="hc", bufs=2, align_bytes=64)
                live[("hs", b)] = st.tile([P, KP, TB], U8, name="hs", tag="hs", bufs=2, align_bytes=64)
            hg = live.pop(("hg", b, c))
            nc.vector.quantize_mx(out=live[("hc", b)][:, c, :].bitcast(FP8X4), scales=live[("hs", b)][:, c, :], in_=hg[:])

        def xp(b):
            if not ok(b):
                return
            x = st.tile([P, 2, 4, TB], F32, name="xp", tag="xp", bufs=2)
            for c in range(2):
                pt = live.pop(("tp", "praw", b, c))
                v = pt[:].bitcast(BF16).rearrange("p (u n e) -> p u n e", u=2, e=2)
                for u in range(2):
                    for e in range(2):
                        t = 2 * u + e
                        col = 4 * (2 + c) + t
                        nc.scalar.activation(out=x[:, c, t, :], in_=v[:, u, :, e], func=ACT.Identity,
                                             bias=b2f[:, col:col + 1], scale=1.0)
            live[("xp", b)] = x

        def m1(b, g):
            if not ok(b):
                return
            hc = live[("hc", b)]
            hs = live[("hs", b)]
            for k in range(2):
                pt = bank("s1")
                for h in range(2):
                    c0 = 512 * g + P * (2 * k + h)
                    for c in range(KP):
                        nc.tensor.matmul_mx(out=pt[:, h * TB:(h + 1) * TB],
                                            lhsT=w2c[:, c, c0:c0 + P].bitcast(FP8X4), lhsT_scale=w2s[:, c, c0:c0 + P],
                                            rhs=hc[:, c, :].bitcast(FP8X4), rhs_scale=hs[:, c, :],
                                            start=(c == 0), stop=(c == KP - 1))
                live[("s1", b, g, k)] = pt

        def stt(b, g, k):
            if not ok(b):
                return
            if k == 0:
                live[("sp", b, g)] = st.tile([P, 4, TB], BF16, name="sp", tag="sp", bufs=3)
            sp = live[("sp", b, g)]
            pt = live.pop(("s1", b, g, k))
            for h in range(2):
                t = 2 * k + h
                col = 4 * g + t
                if g == 0:
                    lo = 0
                    while lo < TB:
                        i = (b * TB + lo) // NODES
                        hi = min(TB, (i + 1) * NODES - b * TB)
                        nc.vector.tensor_scalar(out=sp[:, t, lo:hi], in0=pt[:, h * TB + lo:h * TB + hi],
                                                scalar1=negb2[:, col:col + 1], scalar2=xi[:, t, i:i + 1],
                                                op0=ALU.max, op1=ALU.add)
                        lo = hi
                else:
                    if g == 1:
                        off = (b * TB) % NODES
                        x = xj[:, t, off:off + TB]
                    else:
                        x = live[("xp", b)][:, g - 2, t, :]
                    nc.vector.scalar_tensor_tensor(out=sp[:, t, :], in0=pt[:, h * TB:(h + 1) * TB],
                                                   scalar=negb2[:, col:col + 1], in1=x, op0=ALU.max, op1=ALU.add)

        def g0r(b, k):
            if not ok(b):
                return
            if k == 0:
                live[("r0", b)] = st.tile([P, 4, TB], F32, name="r0", tag="f4k", bufs=F4K, align_bytes=64)
            pt = live.pop(("s1", b, 0, k))
            for h in range(2):
                t = 2 * k + h
                nc.scalar.activation(out=live[("r0", b)][:, t, :], in_=pt[:, h * TB:(h + 1) * TB], func=ACT.Relu,
                                     bias=b2f[:, t:t + 1], scale=1.0)

        def g0a(b):
            if not ok(b):
                return
            sp = st.tile([P, 4, TB], BF16, name="sp", tag="sp", bufs=3)
            r0 = live.pop(("r0", b))
            for t in range(4):
                lo = 0
                while lo < TB:
                    i = (b * TB + lo) // NODES
                    hi = min(TB, (i + 1) * NODES - b * TB)
                    nc.scalar.activation(out=sp[:, t, lo:hi], in_=r0[:, t, lo:hi], func=ACT.Identity,
                                         bias=xi[:, t, i:i + 1], scale=1.0)
                    lo = hi
            live[("sp", b, 0)] = sp

        def il(b, g):
            if not ok(b):
                return
            sp = live.pop(("sp", b, g))
            sg = st.tile([P, TB, 4], BF16, name="sg", tag="sg", bufs=3, align_bytes=64)
            nc.scalar.copy(out=sg[:], in_=sp[:].rearrange("p t n -> p n t"))
            live[("sg", b, g)] = sg

        def qs(b, g):
            if not ok(b):
                return
            if g == 0:
                live[("sc", b)] = st.tile([P, NG, TB], U32, name="sc", tag="sc", bufs=4, align_bytes=64)
                live[("ss", b)] = st.tile([P, NG, TB], U8, name="ss", tag="ss", bufs=4, align_bytes=64)
            sg = live.pop(("sg", b, g))
            nc.vector.quantize_mx(out=live[("sc", b)][:, g, :].bitcast(FP8X4), scales=live[("ss", b)][:, g, :],
                                  in_=sg[:].rearrange("p n t -> p (n t)"))

        def m2(b, i):
            if not ok(b):
                return
            sc = live[("sc", b)]
            ss = live[("ss", b)]
            for h in range(2):
                pt = bank("s2")
                for g in range(NG):
                    nc.tensor.matmul_mx(out=pt[:], lhsT=sc[:, g, i * P:(i + 1) * P].bitcast(FP8X4),
                                        lhsT_scale=ss[:, g, i * P:(i + 1) * P],
                                        rhs=woc[:, g, h * 512:(h + 1) * 512].bitcast(FP8X4),
                                        rhs_scale=wos[:, g, h * 512:(h + 1) * 512],
                                        start=(g == 0), stop=(g == NG - 1))
                live[("s2", b, i, h)] = pt

        def i1(b, i, h):
            if not ok(b):
                return
            if h == 0:
                live[("z", b, i)] = st.tile([P, ED], F32, name="z", tag="f4k", bufs=F4K, align_bytes=64)
                live[("zs", b, i)] = st.tile([P, 2], F32, name="zs", tag="zs", bufs=3)
            pt = live.pop(("s2", b, i, h))
            nc.vector.scalar_tensor_tensor(out=live[("z", b, i)][:, h * 512:(h + 1) * 512], in0=pt[:], scalar=1.0,
                                           in1=cbc[:, 0, h * 512:(h + 1) * 512], op0=ALU.mult, op1=ALU.add,
                                           accum_out=live[("zs", b, i)][:, h:h + 1])

        def negmu(b, i):
            if not ok(b):
                return
            nm = st.tile([P, 1], F32, name="nm", tag="nm", bufs=3)
            zs = live.pop(("zs", b, i))
            zj = st.tile([P, 2], F32, name="zj", tag="zj", bufs=2)
            nc.scalar.activation(out=zj[:], in_=zs[:], func=ACT.Identity, scale=-1.0 / ED, accum_out=nm[:])
            live[("nm", b, i)] = nm

        def i3(b, i):
            if not ok(b):
                return
            y = st.tile([P, ED], F32, name="y", tag="f4k", bufs=F4K, align_bytes=64)
            nc.vector.scalar_tensor_tensor(out=y[:], in0=live[("z", b, i)][:], scalar=live[("nm", b, i)][:],
                                           in1=cbc[:, 1, :], op0=ALU.add, op1=ALU.mult)
            live[("y", b, i)] = y

        def sq(b, i):
            if not ok(b):
                return
            junk = st.tile([P, ED], BF16, name="junk", tag="junk", bufs=1)
            ssq = st.tile([P, 1], F32, name="ssq", tag="ssq", bufs=3)
            sd = st.tile([P, 1], F32, name="sd", tag="sd", bufs=3)
            nc.scalar.activation(out=junk[:], in_=live[("z", b, i)][:], func=ACT.Square,
                                 bias=live[("nm", b, i)][:], scale=1.0, accum_out=ssq[:])
            live[("ssq", b, i)] = ssq
            live[("sd", b, i)] = sd

        def sqr(b, i):
            if not ok(b):
                return
            nc.scalar.activation(out=live[("sd", b, i)][:], in_=live.pop(("ssq", b, i))[:], func=ACT.Sqrt, bias=eps[:],
                                 scale=1.0 / ED)

        def qadd(b, i):
            if not ok(b) or ("q", b, i) in live:
                return
            q = st.tile([P, ED], F32, name="q", tag="f4k", bufs=F4K, align_bytes=64)
            nc.vector.tensor_tensor(out=q[:], in0=live.pop(("praw", b, i))[:], in1=cbc[:, 2, :], op=ALU.add)
            live[("q", b, i)] = q

        def rcp(b, i):
            if not ok(b):
                return
            rstd = st.tile([P, 1], F32, name="rstd", tag="rstd", bufs=3)
            nc.vector.reciprocal(out=rstd[:], in_=live.pop(("sd", b, i))[:])
            live[("rstd", b, i)] = rstd

        def fin(b, i):
            if not ok(b):
                return
            rstd = live.pop(("rstd", b, i))
            y = live.pop(("y", b, i))
            nc.vector.scalar_tensor_tensor(out=y[:], in0=y[:], scalar=rstd[:], in1=live.pop(("q", b, i))[:],
                                           op0=ALU.mult, op1=ALU.add)
            r0 = b * TB + i * P
            nc.sync.dma_start(out=out_rows[r0:r0 + P, :], in_=y[:])

        chunks = []
        for g in range(NG):
            for c in range(KP):
                chunks.append((W2, w2c, w2s, c, 512 * g, True))
        for c in range(NG):
            for h in range(2):
                chunks.append((Wo, woc, wos, c, 512 * h, False))
        copied = set()
        wnext = [W_AHEAD]

        def w_load(n):
            if n >= len(chunks):
                return
            src, cod, sca, c, c0, perm = chunks[n]
            t = st.tile([P, 4, 512], BF16, name="wraw", tag="f4k", bufs=F4K, align_bytes=64)
            nc.sync.dma_start(out=t[:], in_=src[512 * c:512 * (c + 1), c0:c0 + 512].rearrange("(p j) w -> p j w", j=4))
            live[("wraw", n)] = t

        def w_copy(n):
            if n >= len(chunks):
                return
            src, cod, sca, c, c0, perm = chunks[n]
            raw = live.pop(("wraw", n))
            grp = st.tile([P, 2048], BF16, name="wgrp", tag="f4k", bufs=F4K, align_bytes=64)
            if perm:
                o = grp[:].rearrange("p (t m j) -> p t m j", t=4, j=4)
                s = raw[:].rearrange("p j (m t) -> p t m j", t=4)
            else:
                o = grp[:].rearrange("p (w j) -> p w j", j=4)
                s = raw[:].rearrange("p j w -> p w j")
            if n % 2 == 0 or n in W_ON_VECTOR:
                nc.vector.tensor_copy(out=o, in_=s)
            else:
                nc.scalar.copy(out=o, in_=s)
            live[("wgrp", n)] = grp
            copied.add(n)
            while (wnext[0] - W_AHEAD) in copied:
                w_load(wnext[0])
                wnext[0] = wnext[0] + 1

        def w_quant(n):
            if n < 0:
                return
            src, cod, sca, c, c0, perm = chunks[n]
            nc.vector.quantize_mx(out=cod[:, c, c0:c0 + 512].bitcast(FP8X4), scales=sca[:, c, c0:c0 + 512],
                                  in_=live.pop(("wgrp", n))[:])

        def step(k):
            w_copy(2 * k + 1)
            w_copy(2 * k)
            w_quant(2 * k - 2)
            w_quant(2 * k - 1)

        load_h(0)
        crow = []
        for v in range(3):
            crow.append(st.tile([P, ED], BF16, name="crow", tag="sp", bufs=3))
            nc.vector.memset(crow[v][:], 0.0)
        nc.gpsimd.memset(xdraw[:], 0.0)
        nc.vector.memset(eps[:], EPS)
        nc.vector.memset(ones[:], 1.0)
        make_identity(nc, ident[:])
        nc.scalar.activation(out=warm[:], in_=eps[:], func=ACT.Sqrt)
        nc.sync.dma_start(out=b2raw[:], in_=b2.rearrange("(g p t) -> p g t", g=NG, t=4))
        nc.sync.dma_start(out=xdraw[0:NODES, :], in_=xd_rows)
        nc.sync.dma_start(out=crow[0][0:1, :], in_=bo.rearrange("(o n) -> o n", o=1))
        nc.sync.dma_start(out=crow[1][0:1, :], in_=ln_out_g.rearrange("(o n) -> o n", o=1))
        nc.sync.dma_start(out=crow[2][0:1, :], in_=ln_out_b.rearrange("(o n) -> o n", o=1))
        for n in range(W_AHEAD):
            w_load(n)

        for v in range(3):
            for h in range(2):
                pt = bank("cb")
                nc.tensor.matmul(out=pt[:], lhsT=ones[:], rhs=crow[v][:, h * 512:(h + 1) * 512],
                                 start=True, stop=True)
                if h == 0:
                    nc.vector.tensor_copy(out=cbc[:, v, h * 512:(h + 1) * 512], in_=pt[:])
                else:
                    nc.scalar.copy(out=cbc[:, v, h * 512:(h + 1) * 512], in_=pt[:])
        nc.vector.tensor_copy(out=b2f[:], in_=b2raw[:].rearrange("p g t -> p (g t)"))
        nc.vector.tensor_scalar(out=negb2[:], in0=b2f[:], scalar1=-1.0, scalar2=None, op0=ALU.mult)
        xt = bank("xt")
        xw = xdraw[:].bitcast(F32)
        for u in range(2):
            nc.tensor.transpose(xt[:, u * P:(u + 1) * P], xw[:, u:256:2], ident[:])
        xv = xt[:, 0:2 * P].bitcast(BF16).rearrange("p (u n e) -> p u n e", u=2, e=2)
        for u in range(2):
            for e in range(2):
                t = 2 * u + e
                nc.scalar.copy(out=xi[:, t, :], in_=xv[:, u, 0:NODES, e])
                nc.scalar.activation(out=xj[:, t, 0:NODES], in_=xv[:, u, 0:NODES, e],
                                     func=ACT.Identity, bias=b2f[:, 4 + t:5 + t], scale=1.0)
        nc.gpsimd.tensor_copy(out=xj[:, :, NODES:2 * NODES], in_=xj[:, :, 0:NODES])
        nc.gpsimd.tensor_copy(out=xj[:, :, 2 * NODES:4 * NODES], in_=xj[:, :, 0:2 * NODES])
        nc.gpsimd.tensor_copy(out=xj[:, :, 4 * NODES:4 * NODES + 16], in_=xj[:, :, 0:16])

        tr1(0)
        tr_bank(0, "hraw", 3)
        for c in range(4):
            cp(0, c)
        step(0)
        for c in range(4):
            qh(0, c)
        step(1)
        load_p(0)
        step(2)
        m1(0, 0)
        tr_bank(0, "praw", 0)
        tr_bank(0, "praw", 1)
        step(3)
        load_h(1)
        g0r(0, 0)
        g0r(0, 1)
        xp(0)
        step(4)
        g0a(0)
        il(0, 0)
        m1(0, 1)
        tr1(1)
        step(5)
        qs(0, 0)
        cp(1, 0)
        cp(1, 1)
        cp(1, 2)
        stt(0, 1, 0)
        stt(0, 1, 1)
        step(6)
        load_p(1)
        il(0, 1)
        m1(0, 2)
        tr2(1)
        qh(1, 0)
        qh(1, 1)
        qh(1, 2)
        step(7)
        qs(0, 1)
        cp(1, 3)
        stt(0, 2, 0)
        stt(0, 2, 1)
        step(8)
        load_h(2)
        il(0, 2)
        m1(0, 3)
        qh(1, 3)
        xp(1)
        qs(0, 2)
        stt(0, 3, 0)

        def late(b):
            k = b - FIRST_LATE
            if k % LATE_EVERY == 0 and 0 <= k // LATE_EVERY < 2 * POSTPONED:
                return (k // LATE_EVERY // 2, k // LATE_EVERY % 2)
            return (-1, 0)

        for b in range(1, NB):
            c = b - 1 if b - 1 >= POSTPONED else -1
            d = b - 2 if b - 2 >= POSTPONED else -1
            eb, ei = late(b)
            fb, fi = late(b - 1)
            load_h(b + 2)
            load_p(b + 1)
            tr1(b + 1)
            stt(b - 1, 3, 1)
            sqr(d, 1)
            rcp(d, 1)
            cp(b + 1, 0)
            i1(fb, fi, 0)
            qadd(c, 0)
            il(b - 1, 3)
            m1(b, 0)
            i1(fb, fi, 1)
            negmu(fb, fi)
            fin(d, 1)
            cp(b + 1, 1)
            sq(fb, fi)
            sqr(fb, fi)
            qs(b - 1, 3)
            g0r(b, 0)
            if b == 1:
                step(9)
            if b == 2:
                step(11)
            qh(b + 1, 0)
            qh(b + 1, 1)
            cp(b + 1, 2)
            i3(fb, fi)
            qadd(c, 1)
            m1(b, 1)
            g0r(b, 1)
            qh(b + 1, 2)
            rcp(fb, fi)
            g0a(b)
            stt(b, 1, 0)
            m2(c, 0)
            fin(fb, fi)
            stt(b, 1, 1)
            il(b, 0)
            i1(c, 0, 0)
            il(b, 1)
            qs(b, 0)
            tr2(b + 1)
            i1(c, 0, 1)
            qs(b, 1)
            negmu(c, 0)
            cp(b + 1, 3)
            i3(c, 0)
            sq(c, 0)
            sqr(c, 0)
            m1(b, 2)
            if b == 1:
                step(10)
            if b == 2:
                step(12)
            qh(b + 1, 3)
            xp(b + 1)
            stt(b, 2, 0)
            rcp(c, 0)
            if b == NB - 1:
                m1(b, 3)
                stt(b, 2, 1)
                fin(c, 0)
                il(b, 2)
                m2(c, 1)
                stt(b, 3, 0)
                qs(b, 2)
                stt(b, 3, 1)
                il(b, 3)
                i1(c, 1, 0)
                qadd(b, 0)
                i1(c, 1, 1)
                qs(b, 3)
                negmu(c, 1)
                sq(c, 1)
                qadd(b, 1)
                i3(c, 1)
            else:
                m2(c, 1)
                stt(b, 2, 1)
                fin(c, 0)
                il(b, 2)
                i1(c, 1, 0)
                m1(b, 3)
                m2(eb, ei)
                i1(c, 1, 1)
                qs(b, 2)
                negmu(c, 1)
                sq(c, 1)
                stt(b, 3, 0)
                qadd(eb, ei)
                i3(c, 1)

        c = NB - 1
        sqr(c - 1, 1)
        rcp(c - 1, 1)
        m2(c, 0)
        m2(c, 1)
        fin(c - 1, 1)
        i1(c, 0, 0)
        i1(c, 0, 1)
        negmu(c, 0)
        i1(c, 1, 0)
        sq(c, 0)
        sqr(c, 0)
        i1(c, 1, 1)
        negmu(c, 1)
        i3(c, 0)
        sq(c, 1)
        sqr(c, 1)
        rcp(c, 0)
        i3(c, 1)
        rcp(c, 1)
        fin(c, 0)
        fin(c, 1)
